import numpy as np
import ml_dtypes


def mxq(x, axis, fmt="e4m3"):
    dtype, down = {"e4m3": (ml_dtypes.float8_e4m3fn, 7), "e5m2": (ml_dtypes.float8_e5m2, 14)}[fmt]
    v = np.moveaxis(np.asarray(x, np.float32).astype(ml_dtypes.bfloat16).astype(np.float64), axis, -1)
    blocks = v.reshape(v.shape[:-1] + (-1, 32))
    amax = np.abs(blocks).max(-1, keepdims=True)
    byte = np.maximum(np.where(amax > 0, np.frexp(amax)[1] - 1 + 127, 0) - down, 1)
    scale = np.exp2(byte - 127.0)
    codes = (blocks / scale).astype(np.float32).astype(dtype).astype(np.float64)
    return np.moveaxis((codes * scale).reshape(v.shape), -1, axis)


WIDE = False


def mx_kscale(k):
    if not WIDE:
        return np.ones(k)
    levels = np.array([20, -20, 10, -10, 0])
    a = np.random.permutation(np.resize(levels, k // 512 * 4)).reshape(k // 512, 4)
    idx = np.arange(k)
    return np.exp2(a[idx // 512, idx % 128 // 32])


BF16 = ml_dtypes.bfloat16


def bf(x):
    return np.asarray(x, np.float32).astype(BF16)


def f64(x):
    return np.asarray(x).astype(np.float64)


B, H, E, V = 512, 1024, 1024, 4096


def sigmoid(v):
    return 1.0 / (1.0 + np.exp(-v))


def draw_w(k, n):
    return bf(np.random.standard_normal((k, n)) / np.sqrt(k))


def gates(x, h, c, w_forget, w_input, w_c_dash, w_forget_c, w_input_c, w_ip_f, w_ip_i, w_ip_c_dash):
    ft = sigmoid(x @ w_ip_f + h @ w_forget + c @ w_forget_c)
    it = sigmoid(x @ w_ip_i + h @ w_input + c @ w_input_c)
    cd = np.tanh(x @ w_ip_c_dash + h @ w_c_dash)
    return ft, it, cd


def setup_inputs():
    u = mx_kscale(H)
    x = bf(np.random.standard_normal((B, E)))
    h = bf(np.random.standard_normal((B, H)))
    c = bf(np.random.standard_normal((B, H)))
    w_forget = draw_w(H, H)
    w_input = draw_w(H, H)
    w_c_dash = draw_w(H, H)
    w_forget_c = draw_w(H, H)
    w_input_c = draw_w(H, H)
    wf0 = draw_w(E, H)
    wi0 = draw_w(E, H)
    wc0 = draw_w(E, H)
    g = bf(np.random.standard_normal((B, H)) * np.exp2(np.random.randint(-12, 1, (B, 1))) * 8.0 * u)
    ft, it, cd = gates(f64(x), f64(h), f64(c), f64(w_forget), f64(w_input), f64(w_c_dash),
                       f64(w_forget_c), f64(w_input_c), f64(wf0), f64(wi0), f64(wc0))
    return {
        "input_data": x,
        "previous_hidden_state": h,
        "previous_c_state": c,
        "w_forget": w_forget,
        "w_input": w_input,
        "w_c_dash": w_c_dash,
        "w_forget_c": w_forget_c,
        "w_input_c": w_input_c,
        "w_ip_f": bf(f64(wf0) / u[None, :]),
        "w_ip_i": bf(f64(wi0) / u[None, :]),
        "w_ip_c_dash": bf(f64(wc0) / u[None, :]),
        "ft": np.asarray(ft, np.float32),
        "it": np.asarray(it, np.float32),
        "ct_dash": np.asarray(cd, np.float32),
        "grad_out": g,
    }


def reference(input_data, previous_hidden_state, previous_c_state, w_forget, w_input, w_c_dash,
              w_forget_c, w_input_c, w_ip_f, w_ip_i, w_ip_c_dash, ft, it, ct_dash, grad_out):
    g = f64(grad_out)
    c = f64(previous_c_state)
    f = f64(ft)
    i = f64(it)
    d = f64(ct_dash)
    dzf = g * (c * f * (1.0 - f))
    dzi = g * (d * i * (1.0 - i))
    dzc = g * (i * (1.0 - d * d))
    out = mxq(dzf, 1, "e5m2") @ mxq(f64(w_ip_f), 1, "e4m3").T
    out = out + (mxq(dzi, 1, "e5m2") @ mxq(f64(w_ip_i), 1, "e4m3").T)
    out = out + (mxq(dzc, 1, "e5m2") @ mxq(f64(w_ip_c_dash), 1, "e4m3").T)
    return out

@@ -1,0 +1,223 @@
+from contextlib import ExitStack
+
+import concourse.mybir as mybir
+from concourse.masks import make_identity
+
+F32 = mybir.dt.float32
+BF16 = mybir.dt.bfloat16
+U32 = mybir.dt.uint32
+U8 = mybir.dt.uint8
+E4M3_X4 = mybir.dt.float8_e4m3fn_x4
+E5M2_X4 = mybir.dt.float8_e5m2_x4
+ALU = mybir.AluOpType
+ACT = mybir.ActivationFunctionType
+
+P = 128
+PACK = 4
+K_PASS = P * PACK
+N_TILE = 512
+
+BATCH, HIDDEN, EMBED = 512, 1024, 1024
+GATES = ("i", "f", "c")
+BATCH_TILES = BATCH // P
+EMBED_HALVES = EMBED // N_TILE
+ROW_TILES = N_TILE // P
+PASSES = HIDDEN // K_PASS
+WORDS = K_PASS // 2
+
+FLOPS = 2 * BATCH * EMBED * len(GATES) * HIDDEN
+BYTES = 2 * BATCH * HIDDEN * 2 + 3 * BATCH * HIDDEN * 4 + 3 * EMBED * HIDDEN * 2 + BATCH * EMBED * 4
+
+
+def tile_lstm_peephole_build_pa_v_kernel(
+    tc,
+    input_data,
+    previous_hidden_state,
+    previous_c_state,
+    w_forget,
+    w_input,
+    w_c_dash,
+    w_forget_c,
+    w_input_c,
+    w_ip_f,
+    w_ip_i,
+    w_ip_c_dash,
+    ft,
+    it,
+    ct_dash,
+    grad_out,
+    out,
+):
+    nc = tc.nc
+    weight_dram = {"f": w_ip_f, "i": w_ip_i, "c": w_ip_c_dash}
+
+    with ExitStack() as ctx:
+        resident = ctx.enter_context(tc.tile_pool(name="resident", bufs=1))
+        vector_temps = ctx.enter_context(tc.tile_pool(name="vector_temps", bufs=1))
+        rotating = ctx.enter_context(tc.tile_pool(name="rotating", bufs=2))
+        results = ctx.enter_context(tc.tile_pool(name="results", bufs=4))
+        transposed = ctx.enter_context(tc.psum_pool(name="transposed", bufs=4))
+        products = ctx.enter_context(tc.psum_pool(name="products", bufs=4))
+
+        ident_f32 = resident.tile([P, P], F32, name="ident_f32")
+        make_identity(nc, ident_f32[:])
+        ident_bf16 = resident.tile([P, P], BF16, name="ident_bf16")
+        make_identity(nc, ident_bf16[:])
+
+        def load(name, shape, dtype, source):
+            tile = resident.tile(shape, dtype, name=name)
+            nc.sync.dma_start(out=tile[:], in_=source)
+            return tile
+
+        batch_in = {}
+
+        def load_batch_tile(m):
+            rows = slice(m * P, (m + 1) * P)
+            batch_in[m] = {
+                "g": load("g%d" % m, [P, HIDDEN], BF16, grad_out[rows, :]),
+                "i": load("i%d" % m, [P, HIDDEN], F32, it[rows, :]),
+                "f": load("f%d" % m, [P, HIDDEN], F32, ft[rows, :]),
+                "d": load("d%d" % m, [P, HIDDEN], F32, ct_dash[rows, :]),
+                "c": load("c%d" % m, [P, HIDDEN], BF16, previous_c_state[rows, :]),
+            }
+
+        weight_in = {}
+
+        def load_weight_half(h):
+            rows = slice(h * N_TILE, (h + 1) * N_TILE)
+            for x in GATES:
+                weight_in[x, h] = load(
+                    "w_%s%d" % (x, h),
+                    [P, ROW_TILES, HIDDEN],
+                    BF16,
+                    weight_dram[x][rows, :].rearrange("(j p) k -> p j k", p=P),
+                )
+
+        load_batch_tile(0)
+        load_weight_half(0)
+        load_batch_tile(1)
+        load_weight_half(1)
+        load_batch_tile(2)
+        load_batch_tile(3)
+
+        weight_codes = {}
+        weight_scales = {}
+
+        def quantise_weight_half(h):
+            for x in GATES:
+                grouped = rotating.tile([P, PASSES, N_TILE, 2], F32, tag="w_grouped", align_bytes=64)
+                for j in range(ROW_TILES):
+                    words = weight_in[x, h][:, j, :].bitcast(F32)
+                    flipped = transposed.tile([P, PASSES, 2, P], F32, tag="flipped")
+                    for c in range(PASSES):
+                        for u in range(2):
+                            first = c * WORDS + u * P
+                            nc.tensor.transpose(
+                                flipped[:, c, u, :], words[:, first : first + P], ident_f32[:]
+                            )
+                    nc.scalar.copy(
+                        out=grouped[:, :, j * P : (j + 1) * P, :],
+                        in_=flipped[:].rearrange("q c u n -> q c n u"),
+                    )
+                codes = resident.tile([P, PASSES, N_TILE], U32, name="wq_%s%d" % (x, h), align_bytes=64)
+                scales = resident.tile([P, PASSES, N_TILE], U8, name="ws_%s%d" % (x, h), align_bytes=64)
+                nc.vector.quantize_mx(
+                    out=codes[:].rearrange("q c n -> q (c n)").bitcast(E4M3_X4),
+                    scales=scales[:].rearrange("q c n -> q (c n)"),
+                    in_=grouped[:].rearrange("q c n u -> q (c n u)").bitcast(BF16),
+                )
+                weight_codes[x, h] = codes
+                weight_scales[x, h] = scales
+
+        grad_codes = {}
+        grad_scales = {}
+
+        def gate_gradients(m):
+            g, i, f = batch_in[m]["g"], batch_in[m]["i"], batch_in[m]["f"]
+            d, c = batch_in[m]["d"], batch_in[m]["c"]
+            d_squared = rotating.tile([P, HIDDEN], F32, tag="d_squared")
+            nc.scalar.activation(out=d_squared[:], in_=d[:], func=ACT.Square)
+
+            minus_gi = vector_temps.tile([P, HIDDEN], F32, tag="minus_gi")
+            nc.vector.scalar_tensor_tensor(
+                out=minus_gi[:], in0=g[:], scalar=-1.0, in1=i[:], op0=ALU.mult, op1=ALU.mult
+            )
+            minus_f1f = vector_temps.tile([P, HIDDEN], F32, tag="minus_f1f")
+            nc.vector.scalar_tensor_tensor(
+                out=minus_f1f[:], in0=f[:], scalar=1.0, in1=f[:], op0=ALU.subtract, op1=ALU.mult
+            )
+            minus_d1i = vector_temps.tile([P, HIDDEN], F32, tag="minus_d1i")
+            nc.vector.scalar_tensor_tensor(
+                out=minus_d1i[:], in0=i[:], scalar=1.0, in1=d[:], op0=ALU.subtract, op1=ALU.mult
+            )
+            minus_gc = vector_temps.tile([P, HIDDEN], F32, tag="minus_gc")
+            nc.vector.scalar_tensor_tensor(
+                out=minus_gc[:], in0=g[:], scalar=-1.0, in1=c[:], op0=ALU.mult, op1=ALU.mult
+            )
+            dz = {}
+            dz["i"] = rotating.tile([P, HIDDEN], BF16, name="dzi")
+            nc.vector.tensor_tensor(out=dz["i"][:], in0=minus_d1i[:], in1=minus_gi[:], op=ALU.mult)
+            dz["f"] = rotating.tile([P, HIDDEN], BF16, name="dzf")
+            nc.vector.tensor_tensor(out=dz["f"][:], in0=minus_f1f[:], in1=minus_gc[:], op=ALU.mult)
+            dz["c"] = rotating.tile([P, HIDDEN], BF16, name="dzc")
+            nc.vector.scalar_tensor_tensor(
+                out=dz["c"][:], in0=d_squared[:], scalar=1.0, in1=minus_gi[:],
+                op0=ALU.subtract, op1=ALU.mult,
+            )
+
+            codes = resident.tile([P, len(GATES), PASSES, P], U32, name="dq%d" % m, align_bytes=64)
+            scales = resident.tile([P, len(GATES), PASSES, P], U8, name="ds%d" % m, align_bytes=64)
+            for slot, x in enumerate(GATES):
+                columns = dz[x][:].rearrange("r (c u q e) -> r c u e q", c=PASSES, u=2, q=P, e=2)
+                grouped = rotating.tile([P, PASSES, P, PACK], BF16, tag="dz_grouped", align_bytes=64)
+                for c in range(PASSES):
+                    flipped = transposed.tile([P, PACK, P], BF16, tag="flipped")
+                    for u in range(2):
+                        for e in range(2):
+                            nc.tensor.transpose(
+                                flipped[:, 2 * u + e, :], columns[:, c, u, e, :], ident_bf16[:]
+                            )
+                    nc.scalar.copy(
+                        out=grouped[:, c, :, :], in_=flipped[:].rearrange("q t r -> q r t")
+                    )
+                nc.vector.quantize_mx(
+                    out=codes[:, slot, :, :].rearrange("q c r -> q (c r)").bitcast(E5M2_X4),
+                    scales=scales[:, slot, :, :].rearrange("q c r -> q (c r)"),
+                    in_=grouped[:].rearrange("q c r t -> q (c r t)"),
+                )
+            grad_codes[m] = codes
+            grad_scales[m] = scales
+
+        def multiply(m, h):
+            product = products.tile([P, N_TILE], F32, tag="product")
+            last = len(GATES) * PASSES - 1
+            for slot, x in enumerate(GATES):
+                for c in range(PASSES):
+                    step = slot * PASSES + c
+                    nc.tensor.matmul_mx(
+                        out=product[:],
+                        lhsT=grad_codes[m][:, slot, c, :].bitcast(E5M2_X4),
+                        lhsT_scale=grad_scales[m][:, slot, c, :],
+                        rhs=weight_codes[x, h][:, c, :].bitcast(E4M3_X4),
+                        rhs_scale=weight_scales[x, h][:, c, :],
+                        start=(step == 0),
+                        stop=(step == last),
+                    )
+            result = results.tile([P, N_TILE], F32, tag="result")
+            nc.scalar.copy(out=result[:], in_=product[:])
+            nc.sync.dma_start(
+                out=out[m * P : (m + 1) * P, h * N_TILE : (h + 1) * N_TILE], in_=result[:]
+            )
+
+        gate_gradients(0)
+        quantise_weight_half(0)
+        multiply(0, 0)
+        gate_gradients(1)
+        quantise_weight_half(1)
+        multiply(1, 0)
+        multiply(0, 1)
+        multiply(1, 1)
+        for m in range(2, BATCH_TILES):
+            gate_gradients(m)
+            for h in range(EMBED_HALVES):
+                multiply(m, h)

@@ -18,12 +18,12 @@ K_PASS = P * PACK
 N_TILE = 512
 
 BATCH, HIDDEN, EMBED = 512, 1024, 1024
-GATES = ("i", "f", "c")
+GATES = ("f", "i", "c")
 BATCH_TILES = BATCH // P
 EMBED_HALVES = EMBED // N_TILE
 ROW_TILES = N_TILE // P
 PASSES = HIDDEN // K_PASS
-WORDS = K_PASS // 2
+PAIRS = PACK // 2
 
 FLOPS = 2 * BATCH * EMBED * len(GATES) * HIDDEN
 BYTES = 2 * BATCH * HIDDEN * 2 + 3 * BATCH * HIDDEN * 4 + 3 * EMBED * HIDDEN * 2 + BATCH * EMBED * 4
@@ -59,10 +59,8 @@ def tile_lstm_peephole_build_pa_v_kernel(
         transposed = ctx.enter_context(tc.psum_pool(name="transposed", bufs=4))
         products = ctx.enter_context(tc.psum_pool(name="products", bufs=4))
 
-        ident_f32 = resident.tile([P, P], F32, name="ident_f32")
-        make_identity(nc, ident_f32[:])
-        ident_bf16 = resident.tile([P, P], BF16, name="ident_bf16")
-        make_identity(nc, ident_bf16[:])
+        identity = resident.tile([P, P], F32, name="identity")
+        make_identity(nc, identity[:])
 
         def load(name, shape, dtype, source):
             tile = resident.tile(shape, dtype, name=name)
@@ -75,69 +73,69 @@ def tile_lstm_peephole_build_pa_v_kernel(
             rows = slice(m * P, (m + 1) * P)
             batch_in[m] = {
                 "g": load("g%d" % m, [P, HIDDEN], BF16, grad_out[rows, :]),
+                "c": load("c%d" % m, [P, HIDDEN], BF16, previous_c_state[rows, :]),
                 "i": load("i%d" % m, [P, HIDDEN], F32, it[rows, :]),
                 "f": load("f%d" % m, [P, HIDDEN], F32, ft[rows, :]),
                 "d": load("d%d" % m, [P, HIDDEN], F32, ct_dash[rows, :]),
-                "c": load("c%d" % m, [P, HIDDEN], BF16, previous_c_state[rows, :]),
             }
 
         weight_in = {}
 
-        def load_weight_half(h):
+        def load_weight_half(x, h):
             rows = slice(h * N_TILE, (h + 1) * N_TILE)
-            for x in GATES:
-                weight_in[x, h] = load(
-                    "w_%s%d" % (x, h),
-                    [P, ROW_TILES, HIDDEN],
-                    BF16,
-                    weight_dram[x][rows, :].rearrange("(j p) k -> p j k", p=P),
-                )
+            weight_in[x, h] = load(
+                "w_%s%d" % (x, h),
+                [P, ROW_TILES, HIDDEN],
+                BF16,
+                weight_dram[x][rows, :].rearrange("(j p) k -> p j k", p=P),
+            )
 
-        load_batch_tile(0)
-        load_weight_half(0)
-        load_batch_tile(1)
-        load_weight_half(1)
-        load_batch_tile(2)
-        load_batch_tile(3)
+        weight_halves = [(x, h) for h in range(EMBED_HALVES) for x in GATES]
+        halves_per_step = 2
+        for m in range(BATCH_TILES):
+            load_batch_tile(m)
+            for x, h in weight_halves[m * halves_per_step : (m + 1) * halves_per_step]:
+                load_weight_half(x, h)
+
+        def flip_rows(rows_bf16, grouped):
+            words = rows_bf16.bitcast(F32)
+            flipped = transposed.tile([P, PASSES, PAIRS, P], F32, tag="flipped")
+            for c in range(PASSES):
+                for u in range(PAIRS):
+                    first = (c * PAIRS + u) * P
+                    nc.tensor.transpose(flipped[:, c, u, :], words[:, first : first + P], identity[:])
+            nc.scalar.copy(out=grouped, in_=flipped[:].rearrange("q c u r -> q c r u"))
 
         weight_codes = {}
         weight_scales = {}
 
-        def quantise_weight_half(h):
-            for x in GATES:
-                grouped = rotating.tile([P, PASSES, N_TILE, 2], F32, tag="w_grouped", align_bytes=64)
-                for j in range(ROW_TILES):
-                    words = weight_in[x, h][:, j, :].bitcast(F32)
-                    flipped = transposed.tile([P, PASSES, 2, P], F32, tag="flipped")
-                    for c in range(PASSES):
-                        for u in range(2):
-                            first = c * WORDS + u * P
-                            nc.tensor.transpose(
-                                flipped[:, c, u, :], words[:, first : first + P], ident_f32[:]
-                            )
-                    nc.scalar.copy(
-                        out=grouped[:, :, j * P : (j + 1) * P, :],
-                        in_=flipped[:].rearrange("q c u n -> q c n u"),
-                    )
-                codes = resident.tile([P, PASSES, N_TILE], U32, name="wq_%s%d" % (x, h), align_bytes=64)
-                scales = resident.tile([P, PASSES, N_TILE], U8, name="ws_%s%d" % (x, h), align_bytes=64)
-                nc.vector.quantize_mx(
-                    out=codes[:].rearrange("q c n -> q (c n)").bitcast(E4M3_X4),
-                    scales=scales[:].rearrange("q c n -> q (c n)"),
-                    in_=grouped[:].rearrange("q c n u -> q (c n u)").bitcast(BF16),
-                )
-                weight_codes[x, h] = codes
-                weight_scales[x, h] = scales
+        def quantise_weight_half(x, h):
+            grouped = rotating.tile([P, PASSES, N_TILE, PAIRS], F32, tag="w_grouped", align_bytes=64)
+            for j in range(ROW_TILES):
+                flip_rows(weight_in[x, h][:, j, :], grouped[:, :, j * P : (j + 1) * P, :])
+            codes = resident.tile([P, PASSES, N_TILE], U32, name="wq_%s%d" % (x, h), align_bytes=64)
+            scales = resident.tile([P, PASSES, N_TILE], U8, name="ws_%s%d" % (x, h), align_bytes=64)
+            nc.vector.quantize_mx(
+                out=codes[:].rearrange("q c n -> q (c n)").bitcast(E4M3_X4),
+                scales=scales[:].rearrange("q c n -> q (c n)"),
+                in_=grouped[:].rearrange("q c n u -> q (c n u)").bitcast(BF16),
+            )
+            weight_codes[x, h] = codes
+            weight_scales[x, h] = scales
 
         grad_codes = {}
         grad_scales = {}
 
         def gate_gradients(m):
-            g, i, f = batch_in[m]["g"], batch_in[m]["i"], batch_in[m]["f"]
-            d, c = batch_in[m]["d"], batch_in[m]["c"]
+            g, c, i = batch_in[m]["g"], batch_in[m]["c"], batch_in[m]["i"]
+            f, d = batch_in[m]["f"], batch_in[m]["d"]
             d_squared = rotating.tile([P, HIDDEN], F32, tag="d_squared")
             nc.scalar.activation(out=d_squared[:], in_=d[:], func=ACT.Square)
 
+            minus_gc = vector_temps.tile([P, HIDDEN], F32, tag="minus_gc")
+            nc.vector.scalar_tensor_tensor(
+                out=minus_gc[:], in0=g[:], scalar=-1.0, in1=c[:], op0=ALU.mult, op1=ALU.mult
+            )
             minus_gi = vector_temps.tile([P, HIDDEN], F32, tag="minus_gi")
             nc.vector.scalar_tensor_tensor(
                 out=minus_gi[:], in0=g[:], scalar=-1.0, in1=i[:], op0=ALU.mult, op1=ALU.mult
@@ -150,15 +148,11 @@ def tile_lstm_peephole_build_pa_v_kernel(
             nc.vector.scalar_tensor_tensor(
                 out=minus_d1i[:], in0=i[:], scalar=1.0, in1=d[:], op0=ALU.subtract, op1=ALU.mult
             )
-            minus_gc = vector_temps.tile([P, HIDDEN], F32, tag="minus_gc")
-            nc.vector.scalar_tensor_tensor(
-                out=minus_gc[:], in0=g[:], scalar=-1.0, in1=c[:], op0=ALU.mult, op1=ALU.mult
-            )
             dz = {}
-            dz["i"] = rotating.tile([P, HIDDEN], BF16, name="dzi")
-            nc.vector.tensor_tensor(out=dz["i"][:], in0=minus_d1i[:], in1=minus_gi[:], op=ALU.mult)
             dz["f"] = rotating.tile([P, HIDDEN], BF16, name="dzf")
             nc.vector.tensor_tensor(out=dz["f"][:], in0=minus_f1f[:], in1=minus_gc[:], op=ALU.mult)
+            dz["i"] = rotating.tile([P, HIDDEN], BF16, name="dzi")
+            nc.vector.tensor_tensor(out=dz["i"][:], in0=minus_d1i[:], in1=minus_gi[:], op=ALU.mult)
             dz["c"] = rotating.tile([P, HIDDEN], BF16, name="dzc")
             nc.vector.scalar_tensor_tensor(
                 out=dz["c"][:], in0=d_squared[:], scalar=1.0, in1=minus_gi[:],
@@ -168,22 +162,12 @@ def tile_lstm_peephole_build_pa_v_kernel(
             codes = resident.tile([P, len(GATES), PASSES, P], U32, name="dq%d" % m, align_bytes=64)
             scales = resident.tile([P, len(GATES), PASSES, P], U8, name="ds%d" % m, align_bytes=64)
             for slot, x in enumerate(GATES):
-                columns = dz[x][:].rearrange("r (c u q e) -> r c u e q", c=PASSES, u=2, q=P, e=2)
-                grouped = rotating.tile([P, PASSES, P, PACK], BF16, tag="dz_grouped", align_bytes=64)
-                for c in range(PASSES):
-                    flipped = transposed.tile([P, PACK, P], BF16, tag="flipped")
-                    for u in range(2):
-                        for e in range(2):
-                            nc.tensor.transpose(
-                                flipped[:, 2 * u + e, :], columns[:, c, u, e, :], ident_bf16[:]
-                            )
-                    nc.scalar.copy(
-                        out=grouped[:, c, :, :], in_=flipped[:].rearrange("q t r -> q r t")
-                    )
+                grouped = rotating.tile([P, PASSES, P, PAIRS], F32, tag="dz_grouped", align_bytes=64)
+                flip_rows(dz[x][:], grouped[:])
                 nc.vector.quantize_mx(
                     out=codes[:, slot, :, :].rearrange("q c r -> q (c r)").bitcast(E5M2_X4),
                     scales=scales[:, slot, :, :].rearrange("q c r -> q (c r)"),
-                    in_=grouped[:].rearrange("q c r t -> q (c r t)"),
+                    in_=grouped[:].rearrange("q c r u -> q (c r u)").bitcast(BF16),
                 )
             grad_codes[m] = codes
             grad_scales[m] = scales
@@ -209,15 +193,16 @@ def tile_lstm_peephole_build_pa_v_kernel(
                 out=out[m * P : (m + 1) * P, h * N_TILE : (h + 1) * N_TILE], in_=result[:]
             )
 
-        gate_gradients(0)
-        quantise_weight_half(0)
-        multiply(0, 0)
-        gate_gradients(1)
-        quantise_weight_half(1)
-        multiply(1, 0)
-        multiply(0, 1)
-        multiply(1, 1)
-        for m in range(2, BATCH_TILES):
+        for m in range(BATCH_TILES):
             gate_gradients(m)
-            for h in range(EMBED_HALVES):
-                multiply(m, h)
+            for x, h in weight_halves[m * halves_per_step : (m + 1) * halves_per_step]:
+                quantise_weight_half(x, h)
+            if m == 1:
+                multiply(0, 0)
+            if m >= 1:
+                multiply(m, 0)
+            if m == 2:
+                multiply(0, 1)
+                multiply(1, 1)
+            if m >= 2:
+                multiply(m, 1)

@@ -55,9 +55,11 @@ def tile_lstm_peephole_build_pa_v_kernel(
         resident = ctx.enter_context(tc.tile_pool(name="resident", bufs=1))
         vector_temps = ctx.enter_context(tc.tile_pool(name="vector_temps", bufs=1))
         rotating = ctx.enter_context(tc.tile_pool(name="rotating", bufs=2))
+        regrouped = ctx.enter_context(tc.tile_pool(name="regrouped", bufs=len(GATES) + 1))
         results = ctx.enter_context(tc.tile_pool(name="results", bufs=4))
         transposed = ctx.enter_context(tc.psum_pool(name="transposed", bufs=4))
         products = ctx.enter_context(tc.psum_pool(name="products", bufs=4))
+        ctx.enter_context(tc.manual_schedule())
 
         identity = resident.tile([P, P], F32, name="identity")
         make_identity(nc, identity[:])
@@ -91,10 +93,13 @@ def tile_lstm_peephole_build_pa_v_kernel(
             )
 
         weight_halves = [(x, h) for h in range(EMBED_HALVES) for x in GATES]
-        halves_per_step = 2
+
+        def halves_of_step(m):
+            return weight_halves[2 * m : 2 * m + 2]
+
         for m in range(BATCH_TILES):
             load_batch_tile(m)
-            for x, h in weight_halves[m * halves_per_step : (m + 1) * halves_per_step]:
+            for x, h in halves_of_step(m):
                 load_weight_half(x, h)
 
         def flip_rows(rows_bf16, grouped):
@@ -106,103 +111,113 @@ def tile_lstm_peephole_build_pa_v_kernel(
                     nc.tensor.transpose(flipped[:, c, u, :], words[:, first : first + P], identity[:])
             nc.scalar.copy(out=grouped, in_=flipped[:].rearrange("q c u r -> q c r u"))
 
+        grad_codes = {}
         weight_codes = {}
-        weight_scales = {}
+        product = {}
 
-        def quantise_weight_half(x, h):
+        def multiply(m, x, h):
+            if x == GATES[0]:
+                product[m, h] = products.tile([P, N_TILE], F32, name="product")
+            grad_words, grad_scales = grad_codes[m, x]
+            weight_words, weight_scales = weight_codes[x, h]
+            for c in range(PASSES):
+                nc.tensor.matmul_mx(
+                    out=product[m, h][:],
+                    lhsT=grad_words[:, c, :].bitcast(E5M2_X4),
+                    lhsT_scale=grad_scales[:, c, :],
+                    rhs=weight_words[:, c, :].bitcast(E4M3_X4),
+                    rhs_scale=weight_scales[:, c, :],
+                    start=(x == GATES[0] and c == 0),
+                    stop=(x == GATES[-1] and c == PASSES - 1),
+                )
+            if x == GATES[-1]:
+                result = results.tile([P, N_TILE], F32, tag="result")
+                nc.scalar.copy(out=result[:], in_=product[m, h][:])
+                nc.sync.dma_start(
+                    out=out[m * P : (m + 1) * P, h * N_TILE : (h + 1) * N_TILE], in_=result[:]
+                )
+
+        weight_grouped = {}
+
+        def flip_weight_half(x, h):
             grouped = rotating.tile([P, PASSES, N_TILE, PAIRS], F32, tag="w_grouped", align_bytes=64)
             for j in range(ROW_TILES):
                 flip_rows(weight_in[x, h][:, j, :], grouped[:, :, j * P : (j + 1) * P, :])
-            codes = resident.tile([P, PASSES, N_TILE], U32, name="wq_%s%d" % (x, h), align_bytes=64)
+            weight_grouped[x, h] = grouped
+
+        def quantise_weight_half(x, h):
+            words = resident.tile([P, PASSES, N_TILE], U32, name="wq_%s%d" % (x, h), align_bytes=64)
             scales = resident.tile([P, PASSES, N_TILE], U8, name="ws_%s%d" % (x, h), align_bytes=64)
             nc.vector.quantize_mx(
-                out=codes[:].rearrange("q c n -> q (c n)").bitcast(E4M3_X4),
+                out=words[:].rearrange("q c n -> q (c n)").bitcast(E4M3_X4),
                 scales=scales[:].rearrange("q c n -> q (c n)"),
-                in_=grouped[:].rearrange("q c n u -> q (c n u)").bitcast(BF16),
+                in_=weight_grouped[x, h][:].rearrange("q c n u -> q (c n u)").bitcast(BF16),
             )
-            weight_codes[x, h] = codes
-            weight_scales[x, h] = scales
+            weight_codes[x, h] = (words, scales)
+            for m in range(BATCH_TILES):
+                if (m, x) in grad_codes:
+                    multiply(m, x, h)
 
-        grad_codes = {}
-        grad_scales = {}
+        grad_grouped = {}
 
-        def gate_gradients(m):
+        def flip_gradient(m, x, dz):
+            grouped = regrouped.tile([P, PASSES, P, PAIRS], F32, tag="dz_grouped", align_bytes=64)
+            flip_rows(dz[:], grouped[:])
+            grad_grouped[m, x] = grouped
+
+        def quantise_gradient(m, x):
+            words = resident.tile([P, PASSES, P], U32, name="dq_%s%d" % (x, m), align_bytes=64)
+            scales = resident.tile([P, PASSES, P], U8, name="ds_%s%d" % (x, m), align_bytes=64)
+            nc.vector.quantize_mx(
+                out=words[:].rearrange("q c r -> q (c r)").bitcast(E5M2_X4),
+                scales=scales[:].rearrange("q c r -> q (c r)"),
+                in_=grad_grouped[m, x][:].rearrange("q c r u -> q (c r u)").bitcast(BF16),
+            )
+            grad_codes[m, x] = (words, scales)
+            for h in range(EMBED_HALVES):
+                if (x, h) in weight_codes:
+                    multiply(m, x, h)
+
+        def affine_product(tile, in0, op0, scalar, in1):
+            nc.vector.scalar_tensor_tensor(
+                out=tile[:], in0=in0[:], scalar=scalar, in1=in1[:], op0=op0, op1=ALU.mult
+            )
+
+        for m in range(BATCH_TILES):
+            waiting_halves = halves_of_step(m - 1) if m > 0 else []
             g, c, i = batch_in[m]["g"], batch_in[m]["c"], batch_in[m]["i"]
             f, d = batch_in[m]["f"], batch_in[m]["d"]
             d_squared = rotating.tile([P, HIDDEN], F32, tag="d_squared")
             nc.scalar.activation(out=d_squared[:], in_=d[:], func=ACT.Square)
 
             minus_gc = vector_temps.tile([P, HIDDEN], F32, tag="minus_gc")
-            nc.vector.scalar_tensor_tensor(
-                out=minus_gc[:], in0=g[:], scalar=-1.0, in1=c[:], op0=ALU.mult, op1=ALU.mult
-            )
+            affine_product(minus_gc, g, ALU.mult, -1.0, c)
             minus_gi = vector_temps.tile([P, HIDDEN], F32, tag="minus_gi")
-            nc.vector.scalar_tensor_tensor(
-                out=minus_gi[:], in0=g[:], scalar=-1.0, in1=i[:], op0=ALU.mult, op1=ALU.mult
-            )
+            affine_product(minus_gi, g, ALU.mult, -1.0, i)
+            if m > 0:
+                for x in GATES:
+                    quantise_gradient(m - 1, x)
             minus_f1f = vector_temps.tile([P, HIDDEN], F32, tag="minus_f1f")
-            nc.vector.scalar_tensor_tensor(
-                out=minus_f1f[:], in0=f[:], scalar=1.0, in1=f[:], op0=ALU.subtract, op1=ALU.mult
-            )
-            minus_d1i = vector_temps.tile([P, HIDDEN], F32, tag="minus_d1i")
-            nc.vector.scalar_tensor_tensor(
-                out=minus_d1i[:], in0=i[:], scalar=1.0, in1=d[:], op0=ALU.subtract, op1=ALU.mult
-            )
-            dz = {}
-            dz["f"] = rotating.tile([P, HIDDEN], BF16, name="dzf")
-            nc.vector.tensor_tensor(out=dz["f"][:], in0=minus_f1f[:], in1=minus_gc[:], op=ALU.mult)
-            dz["i"] = rotating.tile([P, HIDDEN], BF16, name="dzi")
-            nc.vector.tensor_tensor(out=dz["i"][:], in0=minus_d1i[:], in1=minus_gi[:], op=ALU.mult)
-            dz["c"] = rotating.tile([P, HIDDEN], BF16, name="dzc")
-            nc.vector.scalar_tensor_tensor(
-                out=dz["c"][:], in0=d_squared[:], scalar=1.0, in1=minus_gi[:],
-                op0=ALU.subtract, op1=ALU.mult,
-            )
-
-            codes = resident.tile([P, len(GATES), PASSES, P], U32, name="dq%d" % m, align_bytes=64)
-            scales = resident.tile([P, len(GATES), PASSES, P], U8, name="ds%d" % m, align_bytes=64)
-            for slot, x in enumerate(GATES):
-                grouped = rotating.tile([P, PASSES, P, PAIRS], F32, tag="dz_grouped", align_bytes=64)
-                flip_rows(dz[x][:], grouped[:])
-                nc.vector.quantize_mx(
-                    out=codes[:, slot, :, :].rearrange("q c r -> q (c r)").bitcast(E5M2_X4),
-                    scales=scales[:, slot, :, :].rearrange("q c r -> q (c r)"),
-                    in_=grouped[:].rearrange("q c r u -> q (c r u)").bitcast(BF16),
-                )
-            grad_codes[m] = codes
-            grad_scales[m] = scales
-
-        def multiply(m, h):
-            product = products.tile([P, N_TILE], F32, tag="product")
-            last = len(GATES) * PASSES - 1
-            for slot, x in enumerate(GATES):
-                for c in range(PASSES):
-                    step = slot * PASSES + c
-                    nc.tensor.matmul_mx(
-                        out=product[:],
-                        lhsT=grad_codes[m][:, slot, c, :].bitcast(E5M2_X4),
-                        lhsT_scale=grad_scales[m][:, slot, c, :],
-                        rhs=weight_codes[x, h][:, c, :].bitcast(E4M3_X4),
-                        rhs_scale=weight_scales[x, h][:, c, :],
-                        start=(step == 0),
-                        stop=(step == last),
-                    )
-            result = results.tile([P, N_TILE], F32, tag="result")
-            nc.scalar.copy(out=result[:], in_=product[:])
-            nc.sync.dma_start(
-                out=out[m * P : (m + 1) * P, h * N_TILE : (h + 1) * N_TILE], in_=result[:]
-            )
-
-        for m in range(BATCH_TILES):
-            gate_gradients(m)
-            for x, h in weight_halves[m * halves_per_step : (m + 1) * halves_per_step]:
+            affine_product(minus_f1f, f, ALU.subtract, 1.0, f)
+            for x, h in waiting_halves[:1]:
                 quantise_weight_half(x, h)
-            if m == 1:
-                multiply(0, 0)
-            if m >= 1:
-                multiply(m, 0)
-            if m == 2:
-                multiply(0, 1)
-                multiply(1, 1)
-            if m >= 2:
-                multiply(m, 1)
+            minus_d1i = vector_temps.tile([P, HIDDEN], F32, tag="minus_d1i")
+            affine_product(minus_d1i, i, ALU.subtract, 1.0, d)
+            for x, h in waiting_halves[1:]:
+                quantise_weight_half(x, h)
+
+            dzf = rotating.tile([P, HIDDEN], BF16, tag="dzf")
+            nc.vector.tensor_tensor(out=dzf[:], in0=minus_f1f[:], in1=minus_gc[:], op=ALU.mult)
+            flip_gradient(m, "f", dzf)
+            for x, h in halves_of_step(m)[:1]:
+                flip_weight_half(x, h)
+            dzi = rotating.tile([P, HIDDEN], BF16, tag="dzi")
+            nc.vector.tensor_tensor(out=dzi[:], in0=minus_d1i[:], in1=minus_gi[:], op=ALU.mult)
+            flip_gradient(m, "i", dzi)
+            dzc = rotating.tile([P, HIDDEN], BF16, tag="dzc")
+            affine_product(dzc, d_squared, ALU.subtract, 1.0, minus_gi)
+            flip_gradient(m, "c", dzc)
+            for x, h in halves_of_step(m)[1:]:
+                flip_weight_half(x, h)
+        for x in GATES:
+            quantise_gradient(BATCH_TILES - 1, x)

@@ -89,7 +89,7 @@ def tile_lstm_peephole_build_pa_v_kernel(
                 "w_%s%d" % (x, h),
                 [P, ROW_TILES, HIDDEN],
                 BF16,
-                weight_dram[x][rows, :].rearrange("(j p) k -> p j k", p=P),
+                weight_dram[x][rows, :].rearrange("(p j) k -> p j k", p=P),
             )
 
         weight_halves = [(x, h) for h in range(EMBED_HALVES) for x in GATES]
@@ -132,7 +132,10 @@ def tile_lstm_peephole_build_pa_v_kernel(
                 )
             if x == GATES[-1]:
                 result = results.tile([P, N_TILE], F32, tag="result")
-                nc.scalar.copy(out=result[:], in_=product[m, h][:])
+                nc.scalar.copy(
+                    out=result[:].rearrange("r (p j) -> r p j", j=ROW_TILES),
+                    in_=product[m, h][:].rearrange("r (j p) -> r p j", j=ROW_TILES),
+                )
                 nc.sync.dma_start(
                     out=out[m * P : (m + 1) * P, h * N_TILE : (h + 1) * N_TILE], in_=result[:]
                 )

@@ -89,7 +89,7 @@ def tile_lstm_peephole_build_pa_v_kernel(
                 "w_%s%d" % (x, h),
                 [P, ROW_TILES, HIDDEN],
                 BF16,
-                weight_dram[x][rows, :].rearrange("(p j) k -> p j k", p=P),
+                weight_dram[x][rows, :].rearrange("(j p) k -> p j k", p=P),
             )
 
         weight_halves = [(x, h) for h in range(EMBED_HALVES) for x in GATES]
@@ -132,10 +132,7 @@ def tile_lstm_peephole_build_pa_v_kernel(
                 )
             if x == GATES[-1]:
                 result = results.tile([P, N_TILE], F32, tag="result")
-                nc.scalar.copy(
-                    out=result[:].rearrange("r (p j) -> r p j", j=ROW_TILES),
-                    in_=product[m, h][:].rearrange("r (j p) -> r p j", j=ROW_TILES),
-                )
+                nc.scalar.copy(out=result[:], in_=product[m, h][:])
                 nc.sync.dma_start(
                     out=out[m * P : (m + 1) * P, h * N_TILE : (h + 1) * N_TILE], in_=result[:]
                 )
@@ -197,30 +194,30 @@ def tile_lstm_peephole_build_pa_v_kernel(
             affine_product(minus_gc, g, ALU.mult, -1.0, c)
             minus_gi = vector_temps.tile([P, HIDDEN], F32, tag="minus_gi")
             affine_product(minus_gi, g, ALU.mult, -1.0, i)
-            if m > 0:
-                for x in GATES:
-                    quantise_gradient(m - 1, x)
             minus_f1f = vector_temps.tile([P, HIDDEN], F32, tag="minus_f1f")
             affine_product(minus_f1f, f, ALU.subtract, 1.0, f)
-            for x, h in waiting_halves[:1]:
-                quantise_weight_half(x, h)
+            if m > 0:
+                quantise_gradient(m - 1, "c")
             minus_d1i = vector_temps.tile([P, HIDDEN], F32, tag="minus_d1i")
             affine_product(minus_d1i, i, ALU.subtract, 1.0, d)
-            for x, h in waiting_halves[1:]:
+            for x, h in waiting_halves[:1]:
                 quantise_weight_half(x, h)
 
             dzf = rotating.tile([P, HIDDEN], BF16, tag="dzf")
             nc.vector.tensor_tensor(out=dzf[:], in0=minus_f1f[:], in1=minus_gc[:], op=ALU.mult)
             flip_gradient(m, "f", dzf)
-            for x, h in halves_of_step(m)[:1]:
-                flip_weight_half(x, h)
+            for x, h in waiting_halves[1:]:
+                quantise_weight_half(x, h)
             dzi = rotating.tile([P, HIDDEN], BF16, tag="dzi")
             nc.vector.tensor_tensor(out=dzi[:], in0=minus_d1i[:], in1=minus_gi[:], op=ALU.mult)
             flip_gradient(m, "i", dzi)
+            for x, h in halves_of_step(m)[:1]:
+                flip_weight_half(x, h)
             dzc = rotating.tile([P, HIDDEN], BF16, tag="dzc")
             affine_product(dzc, d_squared, ALU.subtract, 1.0, minus_gi)
             flip_gradient(m, "c", dzc)
             for x, h in halves_of_step(m)[1:]:
                 flip_weight_half(x, h)
-        for x in GATES:
-            quantise_gradient(BATCH_TILES - 1, x)
+            quantise_gradient(m, "f")
+            quantise_gradient(m, "i")
+        quantise_gradient(BATCH_TILES - 1, "c")

@@ -187,6 +187,7 @@ def tile_lstm_peephole_build_pa_v_kernel(
             waiting_halves = halves_of_step(m - 1) if m > 0 else []
             g, c, i = batch_in[m]["g"], batch_in[m]["c"], batch_in[m]["i"]
             f, d = batch_in[m]["f"], batch_in[m]["d"]
+            nc.scalar.activation(out=f[:], in_=f[:], func=ACT.Square, bias=-0.5)
             d_squared = rotating.tile([P, HIDDEN], F32, tag="d_squared")
             nc.scalar.activation(out=d_squared[:], in_=d[:], func=ACT.Square)
 
@@ -194,8 +195,6 @@ def tile_lstm_peephole_build_pa_v_kernel(
             affine_product(minus_gc, g, ALU.mult, -1.0, c)
             minus_gi = vector_temps.tile([P, HIDDEN], F32, tag="minus_gi")
             affine_product(minus_gi, g, ALU.mult, -1.0, i)
-            minus_f1f = vector_temps.tile([P, HIDDEN], F32, tag="minus_f1f")
-            affine_product(minus_f1f, f, ALU.subtract, 1.0, f)
             if m > 0:
                 quantise_gradient(m - 1, "c")
             minus_d1i = vector_temps.tile([P, HIDDEN], F32, tag="minus_d1i")
@@ -204,7 +203,7 @@ def tile_lstm_peephole_build_pa_v_kernel(
                 quantise_weight_half(x, h)
 
             dzf = rotating.tile([P, HIDDEN], BF16, tag="dzf")
-            nc.vector.tensor_tensor(out=dzf[:], in0=minus_f1f[:], in1=minus_gc[:], op=ALU.mult)
+            affine_product(dzf, f, ALU.subtract, 0.25, minus_gc)
             flip_gradient(m, "f", dzf)
             for x, h in waiting_halves[1:]:
                 quantise_weight_half(x, h)

@@ -18,7 +18,7 @@ K_PASS = P * PACK
 N_TILE = 512
 
 BATCH, HIDDEN, EMBED = 512, 1024, 1024
-GATES = ("f", "i", "c")
+GATES = ("i", "f", "c")
 BATCH_TILES = BATCH // P
 EMBED_HALVES = EMBED // N_TILE
 ROW_TILES = N_TILE // P
@@ -77,8 +77,8 @@ def tile_lstm_peephole_build_pa_v_kernel(
                 "g": load("g%d" % m, [P, HIDDEN], BF16, grad_out[rows, :]),
                 "c": load("c%d" % m, [P, HIDDEN], BF16, previous_c_state[rows, :]),
                 "i": load("i%d" % m, [P, HIDDEN], F32, it[rows, :]),
-                "f": load("f%d" % m, [P, HIDDEN], F32, ft[rows, :]),
                 "d": load("d%d" % m, [P, HIDDEN], F32, ct_dash[rows, :]),
+                "f": load("f%d" % m, [P, HIDDEN], F32, ft[rows, :]),
             }
 
         weight_in = {}
@@ -202,14 +202,14 @@ def tile_lstm_peephole_build_pa_v_kernel(
             for x, h in waiting_halves[:1]:
                 quantise_weight_half(x, h)
 
-            dzf = rotating.tile([P, HIDDEN], BF16, tag="dzf")
-            affine_product(dzf, f, ALU.subtract, 0.25, minus_gc)
-            flip_gradient(m, "f", dzf)
-            for x, h in waiting_halves[1:]:
-                quantise_weight_half(x, h)
             dzi = rotating.tile([P, HIDDEN], BF16, tag="dzi")
             nc.vector.tensor_tensor(out=dzi[:], in0=minus_d1i[:], in1=minus_gi[:], op=ALU.mult)
             flip_gradient(m, "i", dzi)
+            for x, h in waiting_halves[1:]:
+                quantise_weight_half(x, h)
+            dzf = rotating.tile([P, HIDDEN], BF16, tag="dzf")
+            affine_product(dzf, f, ALU.subtract, 0.25, minus_gc)
+            flip_gradient(m, "f", dzf)
             for x, h in halves_of_step(m)[:1]:
                 flip_weight_half(x, h)
             dzc = rotating.tile([P, HIDDEN], BF16, tag="dzc")
@@ -217,6 +217,6 @@ def tile_lstm_peephole_build_pa_v_kernel(
             flip_gradient(m, "c", dzc)
             for x, h in halves_of_step(m)[1:]:
                 flip_weight_half(x, h)
-            quantise_gradient(m, "f")
             quantise_gradient(m, "i")
+            quantise_gradient(m, "f")
         quantise_gradient(BATCH_TILES - 1, "c")

@@ -139,11 +139,12 @@ def tile_lstm_peephole_build_pa_v_kernel(
 
         weight_grouped = {}
 
-        def flip_weight_half(x, h):
-            grouped = rotating.tile([P, PASSES, N_TILE, PAIRS], F32, tag="w_grouped", align_bytes=64)
-            for j in range(ROW_TILES):
-                flip_rows(weight_in[x, h][:, j, :], grouped[:, :, j * P : (j + 1) * P, :])
-            weight_grouped[x, h] = grouped
+        def flip_weight_rows(x, h, row_tiles):
+            if (x, h) not in weight_grouped:
+                grouped = rotating.tile([P, PASSES, N_TILE, PAIRS], F32, tag="w_grouped", align_bytes=64)
+                weight_grouped[x, h] = grouped
+            for j in row_tiles:
+                flip_rows(weight_in[x, h][:, j, :], weight_grouped[x, h][:, :, j * P : (j + 1) * P, :])
 
         def quantise_weight_half(x, h):
             words = resident.tile([P, PASSES, N_TILE], U32, name="wq_%s%d" % (x, h), align_bytes=64)
@@ -205,18 +206,20 @@ def tile_lstm_peephole_build_pa_v_kernel(
             dzi = rotating.tile([P, HIDDEN], BF16, tag="dzi")
             nc.vector.tensor_tensor(out=dzi[:], in0=minus_d1i[:], in1=minus_gi[:], op=ALU.mult)
             flip_gradient(m, "i", dzi)
+            for x, h in halves_of_step(m)[:1]:
+                flip_weight_rows(x, h, range(ROW_TILES // 2))
             for x, h in waiting_halves[1:]:
                 quantise_weight_half(x, h)
             dzf = rotating.tile([P, HIDDEN], BF16, tag="dzf")
             affine_product(dzf, f, ALU.subtract, 0.25, minus_gc)
             flip_gradient(m, "f", dzf)
             for x, h in halves_of_step(m)[:1]:
-                flip_weight_half(x, h)
+                flip_weight_rows(x, h, range(ROW_TILES // 2, ROW_TILES))
             dzc = rotating.tile([P, HIDDEN], BF16, tag="dzc")
             affine_product(dzc, d_squared, ALU.subtract, 1.0, minus_gi)
             flip_gradient(m, "c", dzc)
             for x, h in halves_of_step(m)[1:]:
-                flip_weight_half(x, h)
+                flip_weight_rows(x, h, range(ROW_TILES))
             quantise_gradient(m, "i")
             quantise_gradient(m, "f")
         quantise_gradient(BATCH_TILES - 1, "c")

@@ -89,7 +89,7 @@ def tile_lstm_peephole_build_pa_v_kernel(
                 "w_%s%d" % (x, h),
                 [P, ROW_TILES, HIDDEN],
                 BF16,
-                weight_dram[x][rows, :].rearrange("(j p) k -> p j k", p=P),
+                weight_dram[x][rows, :].rearrange("(p j) k -> p j k", j=ROW_TILES),
             )
 
         weight_halves = [(x, h) for h in range(EMBED_HALVES) for x in GATES]
@@ -132,7 +132,10 @@ def tile_lstm_peephole_build_pa_v_kernel(
                 )
             if x == GATES[-1]:
                 result = results.tile([P, N_TILE], F32, tag="result")
-                nc.scalar.copy(out=result[:], in_=product[m, h][:])
+                nc.scalar.copy(
+                    out=result[:].rearrange("b (p j) -> b p j", j=ROW_TILES),
+                    in_=product[m, h][:].rearrange("b (j p) -> b p j", j=ROW_TILES),
+                )
                 nc.sync.dma_start(
                     out=out[m * P : (m + 1) * P, h * N_TILE : (h + 1) * N_TILE], in_=result[:]
                 )

@@ -18,7 +18,7 @@ K_PASS = P * PACK
 N_TILE = 512
 
 BATCH, HIDDEN, EMBED = 512, 1024, 1024
-GATES = ("i", "f", "c")
+GATES = ("i", "c", "f")
 BATCH_TILES = BATCH // P
 EMBED_HALVES = EMBED // N_TILE
 ROW_TILES = N_TILE // P
@@ -191,16 +191,16 @@ def tile_lstm_peephole_build_pa_v_kernel(
             waiting_halves = halves_of_step(m - 1) if m > 0 else []
             g, c, i = batch_in[m]["g"], batch_in[m]["c"], batch_in[m]["i"]
             f, d = batch_in[m]["f"], batch_in[m]["d"]
-            nc.scalar.activation(out=f[:], in_=f[:], func=ACT.Square, bias=-0.5)
             d_squared = rotating.tile([P, HIDDEN], F32, tag="d_squared")
             nc.scalar.activation(out=d_squared[:], in_=d[:], func=ACT.Square)
+            nc.scalar.activation(out=f[:], in_=f[:], func=ACT.Square, bias=-0.5)
 
             minus_gc = vector_temps.tile([P, HIDDEN], F32, tag="minus_gc")
             affine_product(minus_gc, g, ALU.mult, -1.0, c)
             minus_gi = vector_temps.tile([P, HIDDEN], F32, tag="minus_gi")
             affine_product(minus_gi, g, ALU.mult, -1.0, i)
             if m > 0:
-                quantise_gradient(m - 1, "c")
+                quantise_gradient(m - 1, "f")
             minus_d1i = vector_temps.tile([P, HIDDEN], F32, tag="minus_d1i")
             affine_product(minus_d1i, i, ALU.subtract, 1.0, d)
             for x, h in waiting_halves[:1]:
@@ -213,16 +213,16 @@ def tile_lstm_peephole_build_pa_v_kernel(
                 flip_weight_rows(x, h, range(ROW_TILES // 2))
             for x, h in waiting_halves[1:]:
                 quantise_weight_half(x, h)
-            dzf = rotating.tile([P, HIDDEN], BF16, tag="dzf")
-            affine_product(dzf, f, ALU.subtract, 0.25, minus_gc)
-            flip_gradient(m, "f", dzf)
-            for x, h in halves_of_step(m)[:1]:
-                flip_weight_rows(x, h, range(ROW_TILES // 2, ROW_TILES))
             dzc = rotating.tile([P, HIDDEN], BF16, tag="dzc")
             affine_product(dzc, d_squared, ALU.subtract, 1.0, minus_gi)
             flip_gradient(m, "c", dzc)
+            for x, h in halves_of_step(m)[:1]:
+                flip_weight_rows(x, h, range(ROW_TILES // 2, ROW_TILES))
+            dzf = rotating.tile([P, HIDDEN], BF16, tag="dzf")
+            affine_product(dzf, f, ALU.subtract, 0.25, minus_gc)
+            flip_gradient(m, "f", dzf)
             for x, h in halves_of_step(m)[1:]:
                 flip_weight_rows(x, h, range(ROW_TILES))
             quantise_gradient(m, "i")
-            quantise_gradient(m, "f")
-        quantise_gradient(BATCH_TILES - 1, "c")
+            quantise_gradient(m, "c")
+        quantise_gradient(BATCH_TILES - 1, "f")

from contextlib import ExitStack

import concourse.mybir as mybir
from concourse.masks import make_identity

F32 = mybir.dt.float32
BF16 = mybir.dt.bfloat16
U32 = mybir.dt.uint32
U8 = mybir.dt.uint8
E4M3_X4 = mybir.dt.float8_e4m3fn_x4
E5M2_X4 = mybir.dt.float8_e5m2_x4
ALU = mybir.AluOpType
ACT = mybir.ActivationFunctionType

P = 128
PACK = 4
K_PASS = P * PACK
N_TILE = 512

BATCH, HIDDEN, EMBED = 512, 1024, 1024
GATES = ("i", "c", "f")
BATCH_TILES = BATCH // P
EMBED_HALVES = EMBED // N_TILE
ROW_TILES = N_TILE // P
PASSES = HIDDEN // K_PASS
PAIRS = PACK // 2

FLOPS = 2 * BATCH * EMBED * len(GATES) * HIDDEN
BYTES = 2 * BATCH * HIDDEN * 2 + 3 * BATCH * HIDDEN * 4 + 3 * EMBED * HIDDEN * 2 + BATCH * EMBED * 4


def tile_lstm_peephole_build_pa_v_kernel(
    tc,
    input_data,
    previous_hidden_state,
    previous_c_state,
    w_forget,
    w_input,
    w_c_dash,
    w_forget_c,
    w_input_c,
    w_ip_f,
    w_ip_i,
    w_ip_c_dash,
    ft,
    it,
    ct_dash,
    grad_out,
    out,
):
    nc = tc.nc
    weight_dram = {"f": w_ip_f, "i": w_ip_i, "c": w_ip_c_dash}

    with ExitStack() as ctx:
        resident = ctx.enter_context(tc.tile_pool(name="resident", bufs=1))
        vector_temps = ctx.enter_context(tc.tile_pool(name="vector_temps", bufs=1))
        rotating = ctx.enter_context(tc.tile_pool(name="rotating", bufs=2))
        regrouped = ctx.enter_context(tc.tile_pool(name="regrouped", bufs=len(GATES) + 1))
        results = ctx.enter_context(tc.tile_pool(name="results", bufs=4))
        transposed = ctx.enter_context(tc.psum_pool(name="transposed", bufs=4))
        products = ctx.enter_context(tc.psum_pool(name="products", bufs=4))
        ctx.enter_context(tc.manual_schedule())

        identity = resident.tile([P, P], F32, name="identity")
        make_identity(nc, identity[:])

        def load(name, shape, dtype, source):
            tile = resident.tile(shape, dtype, name=name)
            nc.sync.dma_start(out=tile[:], in_=source)
            return tile

        batch_in = {}

        def load_batch_tile(m):
            rows = slice(m * P, (m + 1) * P)
            batch_in[m] = {
                "g": load("g%d" % m, [P, HIDDEN], BF16, grad_out[rows, :]),
                "c": load("c%d" % m, [P, HIDDEN], BF16, previous_c_state[rows, :]),
                "i": load("i%d" % m, [P, HIDDEN], F32, it[rows, :]),
                "d": load("d%d" % m, [P, HIDDEN], F32, ct_dash[rows, :]),
                "f": load("f%d" % m, [P, HIDDEN], F32, ft[rows, :]),
            }

        weight_in = {}

        def load_weight_half(x, h):
            rows = slice(h * N_TILE, (h + 1) * N_TILE)
            weight_in[x, h] = load(
                "w_%s%d" % (x, h),
                [P, ROW_TILES, HIDDEN],
                BF16,
                weight_dram[x][rows, :].rearrange("(p j) k -> p j k", j=ROW_TILES),
            )

        weight_halves = [(x, h) for h in range(EMBED_HALVES) for x in GATES]

        def halves_of_step(m):
            return weight_halves[2 * m : 2 * m + 2]

        for m in range(BATCH_TILES):
            load_batch_tile(m)
            for x, h in halves_of_step(m):
                load_weight_half(x, h)

        def flip_rows(rows_bf16, grouped):
            words = rows_bf16.bitcast(F32)
            flipped = transposed.tile([P, PASSES, PAIRS, P], F32, tag="flipped")
            for c in range(PASSES):
                for u in range(PAIRS):
                    first = (c * PAIRS + u) * P
                    nc.tensor.transpose(flipped[:, c, u, :], words[:, first : first + P], identity[:])
            nc.scalar.copy(out=grouped, in_=flipped[:].rearrange("q c u r -> q c r u"))

        grad_codes = {}
        weight_codes = {}
        product = {}

        def multiply(m, x, h):
            if x == GATES[0]:
                product[m, h] = products.tile([P, N_TILE], F32, name="product")
            grad_words, grad_scales = grad_codes[m, x]
            weight_words, weight_scales = weight_codes[x, h]
            for c in range(PASSES):
                nc.tensor.matmul_mx(
                    out=product[m, h][:],
                    lhsT=grad_words[:, c, :].bitcast(E5M2_X4),
                    lhsT_scale=grad_scales[:, c, :],
                    rhs=weight_words[:, c, :].bitcast(E4M3_X4),
                    rhs_scale=weight_scales[:, c, :],
                    start=(x == GATES[0] and c == 0),
                    stop=(x == GATES[-1] and c == PASSES - 1),
                )
            if x == GATES[-1]:
                result = results.tile([P, N_TILE], F32, tag="result")
                nc.scalar.copy(
                    out=result[:].rearrange("b (p j) -> b p j", j=ROW_TILES),
                    in_=product[m, h][:].rearrange("b (j p) -> b p j", j=ROW_TILES),
                )
                nc.sync.dma_start(
                    out=out[m * P : (m + 1) * P, h * N_TILE : (h + 1) * N_TILE], in_=result[:]
                )

        weight_grouped = {}

        def flip_weight_rows(x, h, row_tiles):
            if (x, h) not in weight_grouped:
                grouped = rotating.tile([P, PASSES, N_TILE, PAIRS], F32, tag="w_grouped", align_bytes=64)
                weight_grouped[x, h] = grouped
            for j in row_tiles:
                flip_rows(weight_in[x, h][:, j, :], weight_grouped[x, h][:, :, j * P : (j + 1) * P, :])

        def quantise_weight_half(x, h):
            words = resident.tile([P, PASSES, N_TILE], U32, name="wq_%s%d" % (x, h), align_bytes=64)
            scales = resident.tile([P, PASSES, N_TILE], U8, name="ws_%s%d" % (x, h), align_bytes=64)
            nc.vector.quantize_mx(
                out=words[:].rearrange("q c n -> q (c n)").bitcast(E4M3_X4),
                scales=scales[:].rearrange("q c n -> q (c n)"),
                in_=weight_grouped[x, h][:].rearrange("q c n u -> q (c n u)").bitcast(BF16),
            )
            weight_codes[x, h] = (words, scales)
            for m in range(BATCH_TILES):
                if (m, x) in grad_codes:
                    multiply(m, x, h)

        grad_grouped = {}

        def flip_gradient(m, x, dz):
            grouped = regrouped.tile([P, PASSES, P, PAIRS], F32, tag="dz_grouped", align_bytes=64)
            flip_rows(dz[:], grouped[:])
            grad_grouped[m, x] = grouped

        def quantise_gradient(m, x):
            words = resident.tile([P, PASSES, P], U32, name="dq_%s%d" % (x, m), align_bytes=64)
            scales = resident.tile([P, PASSES, P], U8, name="ds_%s%d" % (x, m), align_bytes=64)
            nc.vector.quantize_mx(
                out=words[:].rearrange("q c r -> q (c r)").bitcast(E5M2_X4),
                scales=scales[:].rearrange("q c r -> q (c r)"),
                in_=grad_grouped[m, x][:].rearrange("q c r u -> q (c r u)").bitcast(BF16),
            )
            grad_codes[m, x] = (words, scales)
            for h in range(EMBED_HALVES):
                if (x, h) in weight_codes:
                    multiply(m, x, h)

        def affine_product(tile, in0, op0, scalar, in1):
            nc.vector.scalar_tensor_tensor(
                out=tile[:], in0=in0[:], scalar=scalar, in1=in1[:], op0=op0, op1=ALU.mult
            )

        for m in range(BATCH_TILES):
            waiting_halves = halves_of_step(m - 1) if m > 0 else []
            g, c, i = batch_in[m]["g"], batch_in[m]["c"], batch_in[m]["i"]
            f, d = batch_in[m]["f"], batch_in[m]["d"]
            d_squared = rotating.tile([P, HIDDEN], F32, tag="d_squared")
            nc.scalar.activation(out=d_squared[:], in_=d[:], func=ACT.Square)
            nc.scalar.activation(out=f[:], in_=f[:], func=ACT.Square, bias=-0.5)

            minus_gc = vector_temps.tile([P, HIDDEN], F32, tag="minus_gc")
            affine_product(minus_gc, g, ALU.mult, -1.0, c)
            minus_gi = vector_temps.tile([P, HIDDEN], F32, tag="minus_gi")
            affine_product(minus_gi, g, ALU.mult, -1.0, i)
            if m > 0:
                quantise_gradient(m - 1, "f")
            minus_d1i = vector_temps.tile([P, HIDDEN], F32, tag="minus_d1i")
            affine_product(minus_d1i, i, ALU.subtract, 1.0, d)
            for x, h in waiting_halves[:1]:
                quantise_weight_half(x, h)

            dzi = rotating.tile([P, HIDDEN], BF16, tag="dzi")
            nc.vector.tensor_tensor(out=dzi[:], in0=minus_d1i[:], in1=minus_gi[:], op=ALU.mult)
            flip_gradient(m, "i", dzi)
            for x, h in halves_of_step(m)[:1]:
                flip_weight_rows(x, h, range(ROW_TILES // 2))
            for x, h in waiting_halves[1:]:
                quantise_weight_half(x, h)
            dzc = rotating.tile([P, HIDDEN], BF16, tag="dzc")
            affine_product(dzc, d_squared, ALU.subtract, 1.0, minus_gi)
            flip_gradient(m, "c", dzc)
            for x, h in halves_of_step(m)[:1]:
                flip_weight_rows(x, h, range(ROW_TILES // 2, ROW_TILES))
            dzf = rotating.tile([P, HIDDEN], BF16, tag="dzf")
            affine_product(dzf, f, ALU.subtract, 0.25, minus_gc)
            flip_gradient(m, "f", dzf)
            for x, h in halves_of_step(m)[1:]:
                flip_weight_rows(x, h, range(ROW_TILES))
            quantise_gradient(m, "i")
            quantise_gradient(m, "c")
        quantise_gradient(BATCH_TILES - 1, "f")
